import numpy as np
import ml_dtypes


def mxq(x, axis, fmt="e4m3"):
    dtype, down = {"e4m3": (ml_dtypes.float8_e4m3fn, 7), "e5m2": (ml_dtypes.float8_e5m2, 14)}[fmt]
    v = np.moveaxis(np.asarray(x, np.float32).astype(ml_dtypes.bfloat16).astype(np.float64), axis, -1)
    blocks = v.reshape(v.shape[:-1] + (-1, 32))
    amax = np.abs(blocks).max(-1, keepdims=True)
    byte = np.maximum(np.where(amax > 0, np.frexp(amax)[1] - 1 + 127, 0) - down, 1)
    scale = np.exp2(byte - 127.0)
    codes = (blocks / scale).astype(np.float32).astype(dtype).astype(np.float64)
    return np.moveaxis((codes * scale).reshape(v.shape), -1, axis)


WIDE = False


def mx_kscale(k):
    if not WIDE:
        return np.ones(k)
    levels = np.array([10, -10, 5, -5, 0])
    a = np.random.permutation(np.resize(levels, k // 512 * 4)).reshape(k // 512, 4)
    idx = np.arange(k)
    return np.exp2(a[idx // 512, idx % 128 // 32])


BF16 = ml_dtypes.bfloat16


def bf(x):
    return np.asarray(x, np.float32).astype(BF16)


def f64(x):
    return np.asarray(x).astype(np.float64)


B, N, D, H, DH, WS = 1, 1024, 1024, 8, 128, 512
INNER = H * DH
NW = N // WS
BW = B * NW


def elu(u):
    return np.where(u > 0.0, u, np.exp(np.minimum(u, 0.0)) - 1.0)


def heads(t):
    return t.reshape(BW, WS, H, DH).transpose(0, 2, 1, 3)


def setup_inputs():
    s = mx_kscale(D)
    return {"x": bf(np.random.standard_normal((B, N, D)) * s),
            "w_k": bf(np.random.standard_normal((D, INNER)) / np.sqrt(D) / s[:, None]),
            "w_v": bf(np.random.standard_normal((D, INNER)) * 0.3 / np.sqrt(D * WS) / s[:, None])}


def reference(x, w_k, w_v):
    xq = mxq(f64(x).reshape(BW, WS, D), 2, "e4m3")
    k = heads(xq @ mxq(f64(w_k), 0, "e4m3"))
    v = heads(xq @ mxq(f64(w_v), 0, "e4m3"))
    kf = elu(k) + 1.0
    return mxq(kf, 2, "e4m3").transpose(0, 1, 3, 2) @ mxq(v, 2, "e4m3")

@@ -1,0 +1,224 @@
+import concourse.mybir as mybir
+from concourse.masks import make_identity
+
+F32 = mybir.dt.float32
+BF16 = mybir.dt.bfloat16
+U32 = mybir.dt.uint32
+U8 = mybir.dt.uint8
+FP8X4 = mybir.dt.float8_e4m3fn_x4
+ALU = mybir.AluOpType
+ACT = mybir.ActivationFunctionType
+
+P = 128
+PACK = 4
+K_PASS = P * PACK
+
+FEATURES = 1024
+INNER = 1024
+HEAD = 128
+WINDOW = 512
+WINDOWS = 2
+PASSES = FEATURES // K_PASS
+GROUP = 4
+GROUPS = INNER // (GROUP * HEAD)
+GROUP_COLS = GROUP * HEAD
+
+FLOPS = 2 * 2 * WINDOWS * WINDOW * FEATURES * INNER + 2 * WINDOWS * WINDOW * INNER * HEAD
+
+
+def tile_localcontextprocessor_pa_kernel(tc, x, w_k, w_v, out):
+    nc = tc.nc
+    x_rows = x.flatten_outer_dims()
+    weights = (w_k, w_v)
+    K, V = 0, 1
+
+    with tc.tile_pool(name="keep", bufs=1) as keep, tc.tile_pool(name="stage", bufs=2) as stage, tc.tile_pool(
+        name="deep", bufs=4
+    ) as deep, tc.psum_pool(name="banks", bufs=7) as banks, tc.psum_pool(
+        name="context", bufs=1
+    ) as context, tc.manual_schedule():
+        x_tok = [
+            [keep.tile([P, PACK, K_PASS], BF16, name="x_tok%d_%d" % (w, g)) for g in range(PASSES)]
+            for w in range(WINDOWS)
+        ]
+        w_feat = [
+            [
+                [keep.tile([P, PACK, GROUP_COLS], BF16, name="w_feat%d_%d_%d" % (m, g, group)) for group in range(GROUPS)]
+                for g in range(PASSES)
+            ]
+            for m in (K, V)
+        ]
+        x_codes = keep.tile([P, PASSES, WINDOWS, WINDOW], U32, align_bytes=64)
+        x_scales = keep.tile([P, PASSES, WINDOWS, WINDOW], U8, align_bytes=64)
+        w_codes = [keep.tile([P, PASSES, INNER], U32, align_bytes=64, name="w_codes%d" % m) for m in (K, V)]
+        w_scales = [keep.tile([P, PASSES, INNER], U8, align_bytes=64, name="w_scales%d" % m) for m in (K, V)]
+
+        def load_window(w):
+            for g in range(PASSES):
+                feats = slice(g * K_PASS, (g + 1) * K_PASS)
+                nc.sync.dma_start(
+                    out=x_tok[w][g][:],
+                    in_=x_rows[w * WINDOW : (w + 1) * WINDOW, feats].rearrange("(p j) d -> p j d", j=PACK),
+                )
+
+        def load_weights(m, group):
+            cols = slice(group * GROUP_COLS, (group + 1) * GROUP_COLS)
+            for g in range(PASSES):
+                for u in range(2):
+                    first = g * K_PASS + u * 2 * P
+                    nc.sync.dma_start(
+                        out=w_feat[m][g][group][:, 2 * u : 2 * u + 2, :],
+                        in_=weights[m][first : first + 2 * P, cols].rearrange("(q e) c -> q e c", e=2),
+                    )
+
+        def turn_window(w):
+            grouped = []
+            for g in range(PASSES):
+                x_words = x_tok[w][g][:].rearrange("p j d -> p (j d)").bitcast(F32)
+                x_grouped = stage.tile([P, PACK * WINDOW], BF16, align_bytes=64)
+                grouped_words = x_grouped[:].bitcast(F32)
+                for pair in range(2):
+                    turned = banks.tile([P, 2, 2, P], F32, tag="bank")
+                    for a in range(2):
+                        for u in range(2):
+                            first = ((2 * pair + a) * 2 + u) * P
+                            nc.tensor.transpose(turned[:, a, u, :], x_words[:, first : first + P], identity[:])
+                    nc.scalar.copy(
+                        out=grouped_words[:, pair * 4 * P : (pair + 1) * 4 * P].rearrange(
+                            "q (a p u) -> q a p u", a=2, u=2
+                        ),
+                        in_=turned[:].rearrange("q a u p -> q a p u"),
+                    )
+                grouped.append(x_grouped)
+            return grouped
+
+        def quantise_window(w, g, x_grouped):
+            nc.vector.quantize_mx(
+                out=x_codes[:, g, w, :].bitcast(FP8X4), scales=x_scales[:, g, w, :], in_=x_grouped[:]
+            )
+
+        def regroup_weights(m, g, group, copy):
+            w_grouped = deep.tile([P, GROUP_COLS, PACK], BF16, align_bytes=64)
+            copy(
+                out=w_grouped[:].rearrange("q (c i) t -> q c t i", i=4),
+                in_=w_feat[m][g][group][:].rearrange("q t (c i) -> q c t i", i=4),
+            )
+            return w_grouped
+
+        def quantise_weights(m, g, group, w_grouped):
+            cols = slice(group * GROUP_COLS, (group + 1) * GROUP_COLS)
+            nc.vector.quantize_mx(
+                out=w_codes[m][:, g, cols].bitcast(FP8X4),
+                scales=w_scales[m][:, g, cols],
+                in_=w_grouped[:].rearrange("q c t -> q (c t)"),
+            )
+
+        def prepare_weights(m, g, group, copy):
+            quantise_weights(m, g, group, regroup_weights(m, g, group, copy))
+
+        def project(w, m, h):
+            bank = banks.tile([P, PACK, HEAD], F32, tag="bank")
+            cols = slice(h * HEAD, (h + 1) * HEAD)
+            for j in range(PACK):
+                toks = slice(j * P, (j + 1) * P)
+                for g in range(PASSES):
+                    nc.tensor.matmul_mx(
+                        out=bank[:, j, :],
+                        lhsT=x_codes[:, g, w, toks].bitcast(FP8X4),
+                        lhsT_scale=x_scales[:, g, w, toks],
+                        rhs=w_codes[m][:, g, cols].bitcast(FP8X4),
+                        rhs_scale=w_scales[m][:, g, cols],
+                        start=(g == 0),
+                        stop=(g == PASSES - 1),
+                    )
+            return bank[:].rearrange("p j c -> p c j")
+
+        def keys(w, group):
+            kf_grouped = stage.tile([P, GROUP, HEAD, PACK], BF16, align_bytes=64)
+            for i in range(GROUP):
+                k = project(w, K, group * GROUP + i)
+                exp_k = deep.tile([P, HEAD, PACK], BF16)
+                nc.scalar.activation(out=exp_k[:], in_=k, func=ACT.Exp)
+                nc.vector.tensor_scalar_min(out=exp_k[:], in0=exp_k[:], scalar1=1.0)
+                nc.vector.scalar_tensor_tensor(
+                    out=kf_grouped[:, i], in0=k, scalar=1.0, in1=exp_k[:], op0=ALU.add, op1=ALU.max
+                )
+            return kf_grouped
+
+        def values(w, group):
+            v_grouped = stage.tile([P, GROUP, HEAD, PACK], BF16, align_bytes=64)
+            for i in range(GROUP):
+                nc.scalar.copy(out=v_grouped[:, i], in_=project(w, V, group * GROUP + i))
+            return v_grouped
+
+        def quantise_tokens(grouped, name):
+            codes = stage.tile([P, GROUP_COLS], U32, align_bytes=64, name=name + "_codes")
+            scales = stage.tile([P, GROUP_COLS], U8, align_bytes=64, name=name + "_scales")
+            nc.vector.quantize_mx(
+                out=codes[:].bitcast(FP8X4), scales=scales[:], in_=grouped[:].rearrange("p i c j -> p (i c j)")
+            )
+            return codes, scales
+
+        def contexts(w, group, kf, v):
+            ctx = context.tile([P, GROUP, HEAD], F32)
+            for i in range(GROUP):
+                cols = slice(i * HEAD, (i + 1) * HEAD)
+                nc.tensor.matmul_mx(
+                    out=ctx[:, i, :],
+                    lhsT=kf[0][:, cols].bitcast(FP8X4),
+                    lhsT_scale=kf[1][:, cols],
+                    rhs=v[0][:, cols].bitcast(FP8X4),
+                    rhs_scale=v[1][:, cols],
+                    start=True,
+                    stop=True,
+                )
+            ctx_sb = stage.tile([P, GROUP, HEAD], F32)
+            nc.scalar.copy(out=ctx_sb[:], in_=ctx[:])
+            nc.sync.dma_start(
+                out=out[w, group * GROUP : (group + 1) * GROUP].rearrange("h d e -> d h e"), in_=ctx_sb[:]
+            )
+
+        for group in range(GROUPS):
+            load_window(group)
+            for m in (K, V):
+                load_weights(m, group)
+        identity = keep.tile([P, P], F32)
+        make_identity(nc, identity[:])
+
+        x0 = turn_window(0)
+        k0 = regroup_weights(K, 0, 0, nc.vector.tensor_copy)
+        k1 = regroup_weights(K, 1, 0, nc.scalar.copy)
+        quantise_window(0, 0, x0[0])
+        quantise_weights(K, 0, 0, k0)
+        quantise_window(0, 1, x0[1])
+        quantise_weights(K, 1, 0, k1)
+        v0 = regroup_weights(V, 0, 0, nc.vector.tensor_copy)
+        v1 = regroup_weights(V, 1, 0, nc.scalar.copy)
+        quantise_weights(V, 0, 0, v0)
+        quantise_weights(V, 1, 0, v1)
+
+        kf_grouped = keys(0, 0)
+        x1 = turn_window(1)
+        kf = quantise_tokens(kf_grouped, "kf")
+        quantise_window(1, 0, x1[0])
+        quantise_window(1, 1, x1[1])
+        prepare_weights(K, 0, 1, nc.vector.tensor_copy)
+        v = quantise_tokens(values(0, 0), "v")
+        prepare_weights(K, 1, 1, nc.vector.tensor_copy)
+        done = (0, 0, kf, v)
+
+        kf_grouped = keys(1, 0)
+        contexts(*done)
+        kf = quantise_tokens(kf_grouped, "kf")
+        prepare_weights(V, 0, 1, nc.vector.tensor_copy)
+        v = quantise_tokens(values(1, 0), "v")
+        prepare_weights(V, 1, 1, nc.scalar.copy)
+        done = (1, 0, kf, v)
+
+        for w in range(WINDOWS):
+            kf_grouped = keys(w, 1)
+            contexts(*done)
+            kf = quantise_tokens(kf_grouped, "kf")
+            v = quantise_tokens(values(w, 1), "v")
+            done = (w, 1, kf, v)
+        contexts(*done)

@@ -48,10 +48,10 @@ def tile_localcontextprocessor_pa_kernel(tc, x, w_k, w_v, out):
             ]
             for m in (K, V)
         ]
-        x_codes = keep.tile([P, PASSES, WINDOWS, WINDOW], U32, align_bytes=64)
-        x_scales = keep.tile([P, PASSES, WINDOWS, WINDOW], U8, align_bytes=64)
-        w_codes = [keep.tile([P, PASSES, INNER], U32, align_bytes=64, name="w_codes%d" % m) for m in (K, V)]
-        w_scales = [keep.tile([P, PASSES, INNER], U8, align_bytes=64, name="w_scales%d" % m) for m in (K, V)]
+        x_codes = keep.tile([P, WINDOWS, PASSES, WINDOW], U32, align_bytes=64)
+        x_scales = keep.tile([P, WINDOWS, PASSES, WINDOW], U8, align_bytes=64)
+        w_codes = [keep.tile([P, GROUPS, PASSES, GROUP_COLS], U32, align_bytes=64, name="w_codes%d" % m) for m in (K, V)]
+        w_scales = [keep.tile([P, GROUPS, PASSES, GROUP_COLS], U8, align_bytes=64, name="w_scales%d" % m) for m in (K, V)]
 
         def load_window(w):
             for g in range(PASSES):
@@ -72,11 +72,10 @@ def tile_localcontextprocessor_pa_kernel(tc, x, w_k, w_v, out):
                     )
 
         def turn_window(w):
-            grouped = []
+            x_grouped = stage.tile([P, PASSES, PACK * WINDOW], BF16, align_bytes=64)
             for g in range(PASSES):
                 x_words = x_tok[w][g][:].rearrange("p j d -> p (j d)").bitcast(F32)
-                x_grouped = stage.tile([P, PACK * WINDOW], BF16, align_bytes=64)
-                grouped_words = x_grouped[:].bitcast(F32)
+                grouped_words = x_grouped[:, g, :].bitcast(F32)
                 for pair in range(2):
                     turned = banks.tile([P, 2, 2, P], F32, tag="bank")
                     for a in range(2):
@@ -89,66 +88,73 @@ def tile_localcontextprocessor_pa_kernel(tc, x, w_k, w_v, out):
                         ),
                         in_=turned[:].rearrange("q a u p -> q a p u"),
                     )
-                grouped.append(x_grouped)
-            return grouped
+            return x_grouped
 
-        def quantise_window(w, g, x_grouped):
+        def quantise_window(w, x_grouped):
             nc.vector.quantize_mx(
-                out=x_codes[:, g, w, :].bitcast(FP8X4), scales=x_scales[:, g, w, :], in_=x_grouped[:]
+                out=x_codes[:, w].rearrange("q g n -> q (g n)").bitcast(FP8X4),
+                scales=x_scales[:, w].rearrange("q g n -> q (g n)"),
+                in_=x_grouped[:].rearrange("q g n -> q (g n)"),
             )
 
-        def regroup_weights(m, g, group, copy):
-            w_grouped = deep.tile([P, GROUP_COLS, PACK], BF16, align_bytes=64)
+        def regroup_weights(w_grouped, m, g, group, copy):
             copy(
-                out=w_grouped[:].rearrange("q (c i) t -> q c t i", i=4),
+                out=w_grouped[:, g].rearrange("q (c i) t -> q c t i", i=4),
                 in_=w_feat[m][g][group][:].rearrange("q t (c i) -> q c t i", i=4),
             )
-            return w_grouped
 
-        def quantise_weights(m, g, group, w_grouped):
-            cols = slice(group * GROUP_COLS, (group + 1) * GROUP_COLS)
+        def quantise_weights(w_grouped, m, group):
             nc.vector.quantize_mx(
-                out=w_codes[m][:, g, cols].bitcast(FP8X4),
-                scales=w_scales[m][:, g, cols],
-                in_=w_grouped[:].rearrange("q c t -> q (c t)"),
+                out=w_codes[m][:, group].rearrange("q g c -> q (g c)").bitcast(FP8X4),
+                scales=w_scales[m][:, group].rearrange("q g c -> q (g c)"),
+                in_=w_grouped[:].rearrange("q g c t -> q (g c t)"),
             )
 
-        def prepare_weights(m, g, group, copy):
-            quantise_weights(m, g, group, regroup_weights(m, g, group, copy))
-
-        def project(w, m, h):
+        def project(w, m, group, i):
             bank = banks.tile([P, PACK, HEAD], F32, tag="bank")
-            cols = slice(h * HEAD, (h + 1) * HEAD)
+            cols = slice(i * HEAD, (i + 1) * HEAD)
             for j in range(PACK):
                 toks = slice(j * P, (j + 1) * P)
                 for g in range(PASSES):
                     nc.tensor.matmul_mx(
                         out=bank[:, j, :],
-                        lhsT=x_codes[:, g, w, toks].bitcast(FP8X4),
-                        lhsT_scale=x_scales[:, g, w, toks],
-                        rhs=w_codes[m][:, g, cols].bitcast(FP8X4),
-                        rhs_scale=w_scales[m][:, g, cols],
+                        lhsT=x_codes[:, w, g, toks].bitcast(FP8X4),
+                        lhsT_scale=x_scales[:, w, g, toks],
+                        rhs=w_codes[m][:, group, g, cols].bitcast(FP8X4),
+                        rhs_scale=w_scales[m][:, group, g, cols],
                         start=(g == 0),
                         stop=(g == PASSES - 1),
                     )
             return bank[:].rearrange("p j c -> p c j")
 
-        def keys(w, group):
-            kf_grouped = stage.tile([P, GROUP, HEAD, PACK], BF16, align_bytes=64)
+        def project_keys(w, group):
+            heads = []
             for i in range(GROUP):
-                k = project(w, K, group * GROUP + i)
+                k = project(w, K, group, i)
                 exp_k = deep.tile([P, HEAD, PACK], BF16)
                 nc.scalar.activation(out=exp_k[:], in_=k, func=ACT.Exp)
-                nc.vector.tensor_scalar_min(out=exp_k[:], in0=exp_k[:], scalar1=1.0)
+                heads.append((k, exp_k))
+            return heads
+
+        def finish_keys(heads):
+            kf_grouped = stage.tile([P, GROUP, HEAD, PACK], BF16, align_bytes=64)
+
+            def clamp(i):
+                nc.vector.tensor_scalar_min(out=heads[i][1][:], in0=heads[i][1][:], scalar1=1.0)
+
+            clamp(0)
+            for i in range(GROUP):
+                if i + 1 < GROUP:
+                    clamp(i + 1)
                 nc.vector.scalar_tensor_tensor(
-                    out=kf_grouped[:, i], in0=k, scalar=1.0, in1=exp_k[:], op0=ALU.add, op1=ALU.max
+                    out=kf_grouped[:, i], in0=heads[i][0], scalar=1.0, in1=heads[i][1][:], op0=ALU.add, op1=ALU.max
                 )
             return kf_grouped
 
         def values(w, group):
             v_grouped = stage.tile([P, GROUP, HEAD, PACK], BF16, align_bytes=64)
             for i in range(GROUP):
-                nc.scalar.copy(out=v_grouped[:, i], in_=project(w, V, group * GROUP + i))
+                nc.scalar.copy(out=v_grouped[:, i], in_=project(w, V, group, i))
             return v_grouped
 
         def quantise_tokens(grouped, name):
@@ -178,6 +184,10 @@ def tile_localcontextprocessor_pa_kernel(tc, x, w_k, w_v, out):
                 out=out[w, group * GROUP : (group + 1) * GROUP].rearrange("h d e -> d h e"), in_=ctx_sb[:]
             )
 
+        def new_w_grouped():
+            w_grouped = deep.tile([P, PASSES, GROUP_COLS, PACK], BF16, align_bytes=64)
+            return w_grouped
+
         for group in range(GROUPS):
             load_window(group)
             for m in (K, V):
@@ -185,40 +195,44 @@ def tile_localcontextprocessor_pa_kernel(tc, x, w_k, w_v, out):
         identity = keep.tile([P, P], F32)
         make_identity(nc, identity[:])
 
-        x0 = turn_window(0)
-        k0 = regroup_weights(K, 0, 0, nc.vector.tensor_copy)
-        k1 = regroup_weights(K, 1, 0, nc.scalar.copy)
-        quantise_window(0, 0, x0[0])
-        quantise_weights(K, 0, 0, k0)
-        quantise_window(0, 1, x0[1])
-        quantise_weights(K, 1, 0, k1)
-        v0 = regroup_weights(V, 0, 0, nc.vector.tensor_copy)
-        v1 = regroup_weights(V, 1, 0, nc.scalar.copy)
-        quantise_weights(V, 0, 0, v0)
-        quantise_weights(V, 1, 0, v1)
+        x_grouped = turn_window(0)
+        k_first = new_w_grouped()
+        regroup_weights(k_first, K, 0, 0, nc.vector.tensor_copy)
+        regroup_weights(k_first, K, 1, 0, nc.scalar.copy)
+        quantise_window(0, x_grouped)
+        quantise_weights(k_first, K, 0)
+        v_first = new_w_grouped()
+        regroup_weights(v_first, V, 0, 0, nc.vector.tensor_copy)
+        regroup_weights(v_first, V, 1, 0, nc.scalar.copy)
+        k_second = new_w_grouped()
+        regroup_weights(k_second, K, 0, 1, nc.vector.tensor_copy)
+        quantise_weights(v_first, V, 0)
 
-        kf_grouped = keys(0, 0)
-        x1 = turn_window(1)
+        heads = project_keys(0, 0)
+        x_grouped = turn_window(1)
+        kf_grouped = finish_keys(heads)
+        quantise_window(1, x_grouped)
         kf = quantise_tokens(kf_grouped, "kf")
-        quantise_window(1, 0, x1[0])
-        quantise_window(1, 1, x1[1])
-        prepare_weights(K, 0, 1, nc.vector.tensor_copy)
+        regroup_weights(k_second, K, 1, 1, nc.vector.tensor_copy)
         v = quantise_tokens(values(0, 0), "v")
-        prepare_weights(K, 1, 1, nc.vector.tensor_copy)
+        quantise_weights(k_second, K, 1)
         done = (0, 0, kf, v)
 
-        kf_grouped = keys(1, 0)
+        heads = project_keys(1, 0)
         contexts(*done)
+        kf_grouped = finish_keys(heads)
+        v_second = new_w_grouped()
+        regroup_weights(v_second, V, 0, 1, nc.vector.tensor_copy)
+        regroup_weights(v_second, V, 1, 1, nc.scalar.copy)
         kf = quantise_tokens(kf_grouped, "kf")
-        prepare_weights(V, 0, 1, nc.vector.tensor_copy)
         v = quantise_tokens(values(1, 0), "v")
-        prepare_weights(V, 1, 1, nc.scalar.copy)
+        quantise_weights(v_second, V, 1)
         done = (1, 0, kf, v)
 
         for w in range(WINDOWS):
-            kf_grouped = keys(w, 1)
+            heads = project_keys(w, 1)
             contexts(*done)
-            kf = quantise_tokens(kf_grouped, "kf")
+            kf = quantise_tokens(finish_keys(heads), "kf")
             v = quantise_tokens(values(w, 1), "v")
             done = (w, 1, kf, v)
         contexts(*done)

@@ -37,10 +37,7 @@ def tile_localcontextprocessor_pa_kernel(tc, x, w_k, w_v, out):
     ) as deep, tc.psum_pool(name="banks", bufs=7) as banks, tc.psum_pool(
         name="context", bufs=1
     ) as context, tc.manual_schedule():
-        x_tok = [
-            [keep.tile([P, PACK, K_PASS], BF16, name="x_tok%d_%d" % (w, g)) for g in range(PASSES)]
-            for w in range(WINDOWS)
-        ]
+        x_tok = [keep.tile([P, PACK, FEATURES], BF16, name="x_tok%d" % w) for w in range(WINDOWS)]
         w_feat = [
             [
                 [keep.tile([P, PACK, GROUP_COLS], BF16, name="w_feat%d_%d_%d" % (m, g, group)) for group in range(GROUPS)]
@@ -54,12 +51,9 @@ def tile_localcontextprocessor_pa_kernel(tc, x, w_k, w_v, out):
         w_scales = [keep.tile([P, GROUPS, PASSES, GROUP_COLS], U8, align_bytes=64, name="w_scales%d" % m) for m in (K, V)]
 
         def load_window(w):
-            for g in range(PASSES):
-                feats = slice(g * K_PASS, (g + 1) * K_PASS)
-                nc.sync.dma_start(
-                    out=x_tok[w][g][:],
-                    in_=x_rows[w * WINDOW : (w + 1) * WINDOW, feats].rearrange("(p j) d -> p j d", j=PACK),
-                )
+            nc.sync.dma_start(
+                out=x_tok[w][:], in_=x_rows[w * WINDOW : (w + 1) * WINDOW, :].rearrange("(p j) d -> p j d", j=PACK)
+            )
 
         def load_weights(m, group):
             cols = slice(group * GROUP_COLS, (group + 1) * GROUP_COLS)
@@ -73,14 +67,14 @@ def tile_localcontextprocessor_pa_kernel(tc, x, w_k, w_v, out):
 
         def turn_window(w):
             x_grouped = stage.tile([P, PASSES, PACK * WINDOW], BF16, align_bytes=64)
+            x_words = x_tok[w][:].rearrange("p j d -> p (j d)").bitcast(F32)
             for g in range(PASSES):
-                x_words = x_tok[w][g][:].rearrange("p j d -> p (j d)").bitcast(F32)
                 grouped_words = x_grouped[:, g, :].bitcast(F32)
                 for pair in range(2):
                     turned = banks.tile([P, 2, 2, P], F32, tag="bank")
                     for a in range(2):
                         for u in range(2):
-                            first = ((2 * pair + a) * 2 + u) * P
+                            first = (((2 * pair + a) * PASSES + g) * 2 + u) * P
                             nc.tensor.transpose(turned[:, a, u, :], x_words[:, first : first + P], identity[:])
                     nc.scalar.copy(
                         out=grouped_words[:, pair * 4 * P : (pair + 1) * 4 * P].rearrange(
@@ -97,17 +91,19 @@ def tile_localcontextprocessor_pa_kernel(tc, x, w_k, w_v, out):
                 in_=x_grouped[:].rearrange("q g n -> q (g n)"),
             )
 
-        def regroup_weights(w_grouped, m, g, group, copy):
+        def regroup_weights(m, g, group, copy):
+            w_grouped = deep.tile([P, GROUP_COLS, PACK], BF16, align_bytes=64)
             copy(
-                out=w_grouped[:, g].rearrange("q (c i) t -> q c t i", i=4),
+                out=w_grouped[:].rearrange("q (c i) t -> q c t i", i=4),
                 in_=w_feat[m][g][group][:].rearrange("q t (c i) -> q c t i", i=4),
             )
+            return m, g, group, w_grouped
 
-        def quantise_weights(w_grouped, m, group):
+        def quantise_weights(m, g, group, w_grouped):
             nc.vector.quantize_mx(
-                out=w_codes[m][:, group].rearrange("q g c -> q (g c)").bitcast(FP8X4),
-                scales=w_scales[m][:, group].rearrange("q g c -> q (g c)"),
-                in_=w_grouped[:].rearrange("q g c t -> q (g c t)"),
+                out=w_codes[m][:, group, g, :].bitcast(FP8X4),
+                scales=w_scales[m][:, group, g, :],
+                in_=w_grouped[:].rearrange("q c t -> q (c t)"),
             )
 
         def project(w, m, group, i):
@@ -184,9 +180,7 @@ def tile_localcontextprocessor_pa_kernel(tc, x, w_k, w_v, out):
                 out=out[w, group * GROUP : (group + 1) * GROUP].rearrange("h d e -> d h e"), in_=ctx_sb[:]
             )
 
-        def new_w_grouped():
-            w_grouped = deep.tile([P, PASSES, GROUP_COLS, PACK], BF16, align_bytes=64)
-            return w_grouped
+        on_vector, on_scalar = nc.vector.tensor_copy, nc.scalar.copy
 
         for group in range(GROUPS):
             load_window(group)
@@ -196,37 +190,39 @@ def tile_localcontextprocessor_pa_kernel(tc, x, w_k, w_v, out):
         make_identity(nc, identity[:])
 
         x_grouped = turn_window(0)
-        k_first = new_w_grouped()
-        regroup_weights(k_first, K, 0, 0, nc.vector.tensor_copy)
-        regroup_weights(k_first, K, 1, 0, nc.scalar.copy)
+        k0 = regroup_weights(K, 0, 0, on_vector)
+        v0 = regroup_weights(V, 0, 0, on_scalar)
+        k1 = regroup_weights(K, 1, 0, on_vector)
+        quantise_weights(*k0)
         quantise_window(0, x_grouped)
-        quantise_weights(k_first, K, 0)
-        v_first = new_w_grouped()
-        regroup_weights(v_first, V, 0, 0, nc.vector.tensor_copy)
-        regroup_weights(v_first, V, 1, 0, nc.scalar.copy)
-        k_second = new_w_grouped()
-        regroup_weights(k_second, K, 0, 1, nc.vector.tensor_copy)
-        quantise_weights(v_first, V, 0)
+        quantise_weights(*k1)
+        v1 = regroup_weights(V, 1, 0, on_vector)
 
         heads = project_keys(0, 0)
+        quantise_weights(*v0)
+        quantise_weights(*v1)
         x_grouped = turn_window(1)
         kf_grouped = finish_keys(heads)
         quantise_window(1, x_grouped)
         kf = quantise_tokens(kf_grouped, "kf")
-        regroup_weights(k_second, K, 1, 1, nc.vector.tensor_copy)
-        v = quantise_tokens(values(0, 0), "v")
-        quantise_weights(k_second, K, 1)
+        k0 = regroup_weights(K, 0, 1, on_vector)
+        v_grouped = values(0, 0)
+        k1 = regroup_weights(K, 1, 1, on_vector)
+        v = quantise_tokens(v_grouped, "v")
+        quantise_weights(*k0)
         done = (0, 0, kf, v)
 
         heads = project_keys(1, 0)
         contexts(*done)
         kf_grouped = finish_keys(heads)
-        v_second = new_w_grouped()
-        regroup_weights(v_second, V, 0, 1, nc.vector.tensor_copy)
-        regroup_weights(v_second, V, 1, 1, nc.scalar.copy)
+        quantise_weights(*k1)
+        v0 = regroup_weights(V, 0, 1, on_vector)
         kf = quantise_tokens(kf_grouped, "kf")
-        v = quantise_tokens(values(1, 0), "v")
-        quantise_weights(v_second, V, 1)
+        v_grouped = values(1, 0)
+        v1 = regroup_weights(V, 1, 1, on_scalar)
+        quantise_weights(*v0)
+        v = quantise_tokens(v_grouped, "v")
+        quantise_weights(*v1)
         done = (1, 0, kf, v)
 
         for w in range(WINDOWS):

@@ -37,7 +37,9 @@ def tile_localcontextprocessor_pa_kernel(tc, x, w_k, w_v, out):
     ) as deep, tc.psum_pool(name="banks", bufs=7) as banks, tc.psum_pool(
         name="context", bufs=1
     ) as context, tc.manual_schedule():
-        x_tok = [keep.tile([P, PACK, FEATURES], BF16, name="x_tok%d" % w) for w in range(WINDOWS)]
+        x_tok = [
+            [keep.tile([P, 2, FEATURES], BF16, name="x_tok%d_%d" % (w, pair)) for pair in range(2)] for w in range(WINDOWS)
+        ]
         w_feat = [
             [
                 [keep.tile([P, PACK, GROUP_COLS], BF16, name="w_feat%d_%d_%d" % (m, g, group)) for group in range(GROUPS)]
@@ -50,38 +52,35 @@ def tile_localcontextprocessor_pa_kernel(tc, x, w_k, w_v, out):
         w_codes = [keep.tile([P, GROUPS, PASSES, GROUP_COLS], U32, align_bytes=64, name="w_codes%d" % m) for m in (K, V)]
         w_scales = [keep.tile([P, GROUPS, PASSES, GROUP_COLS], U8, align_bytes=64, name="w_scales%d" % m) for m in (K, V)]
 
-        def load_window(w):
-            nc.sync.dma_start(
-                out=x_tok[w][:], in_=x_rows[w * WINDOW : (w + 1) * WINDOW, :].rearrange("(p j) d -> p j d", j=PACK)
-            )
+        def load_tokens(w, pair):
+            window = x_rows[w * WINDOW : (w + 1) * WINDOW, :].rearrange("(p j) d -> p j d", j=PACK)
+            nc.sync.dma_start(out=x_tok[w][pair][:], in_=window[:, 2 * pair : 2 * pair + 2, :])
 
-        def load_weights(m, group):
+        def load_weights(m, g, group):
             cols = slice(group * GROUP_COLS, (group + 1) * GROUP_COLS)
-            for g in range(PASSES):
-                for u in range(2):
-                    first = g * K_PASS + u * 2 * P
-                    nc.sync.dma_start(
-                        out=w_feat[m][g][group][:, 2 * u : 2 * u + 2, :],
-                        in_=weights[m][first : first + 2 * P, cols].rearrange("(q e) c -> q e c", e=2),
-                    )
+            for u in range(2):
+                first = g * K_PASS + u * 2 * P
+                nc.sync.dma_start(
+                    out=w_feat[m][g][group][:, 2 * u : 2 * u + 2, :],
+                    in_=weights[m][first : first + 2 * P, cols].rearrange("(q e) c -> q e c", e=2),
+                )
 
-        def turn_window(w):
-            x_grouped = stage.tile([P, PASSES, PACK * WINDOW], BF16, align_bytes=64)
-            x_words = x_tok[w][:].rearrange("p j d -> p (j d)").bitcast(F32)
+        def turn_tokens(w, pair, x_grouped):
+            x_words = x_tok[w][pair][:].rearrange("p a d -> p (a d)").bitcast(F32)
             for g in range(PASSES):
+                turned = banks.tile([P, 2, 2, P], F32, tag="bank")
+                for a in range(2):
+                    for u in range(2):
+                        first = ((a * PASSES + g) * 2 + u) * P
+                        nc.tensor.transpose(turned[:, a, u, :], x_words[:, first : first + P], identity[:])
                 grouped_words = x_grouped[:, g, :].bitcast(F32)
-                for pair in range(2):
-                    turned = banks.tile([P, 2, 2, P], F32, tag="bank")
-                    for a in range(2):
-                        for u in range(2):
-                            first = (((2 * pair + a) * PASSES + g) * 2 + u) * P
-                            nc.tensor.transpose(turned[:, a, u, :], x_words[:, first : first + P], identity[:])
-                    nc.scalar.copy(
-                        out=grouped_words[:, pair * 4 * P : (pair + 1) * 4 * P].rearrange(
-                            "q (a p u) -> q a p u", a=2, u=2
-                        ),
-                        in_=turned[:].rearrange("q a u p -> q a p u"),
-                    )
+                nc.scalar.copy(
+                    out=grouped_words[:, pair * 4 * P : (pair + 1) * 4 * P].rearrange("q (a p u) -> q a p u", a=2, u=2),
+                    in_=turned[:].rearrange("q a u p -> q a p u"),
+                )
+
+        def new_x_grouped():
+            x_grouped = stage.tile([P, PASSES, PACK * WINDOW], BF16, align_bytes=64)
             return x_grouped
 
         def quantise_window(w, x_grouped):
@@ -182,18 +181,26 @@ def tile_localcontextprocessor_pa_kernel(tc, x, w_k, w_v, out):
 
         on_vector, on_scalar = nc.vector.tensor_copy, nc.scalar.copy
 
-        for group in range(GROUPS):
-            load_window(group)
-            for m in (K, V):
-                load_weights(m, group)
+        for g in range(PASSES):
+            load_tokens(0, g)
+            load_weights(K, g, 0)
+        for g in range(PASSES):
+            load_weights(V, g, 0)
+        for pair in range(2):
+            load_tokens(1, pair)
+        for m in (K, V):
+            for g in range(PASSES):
+                load_weights(m, g, 1)
         identity = keep.tile([P, P], F32)
         make_identity(nc, identity[:])
 
-        x_grouped = turn_window(0)
+        x_grouped = new_x_grouped()
+        turn_tokens(0, 0, x_grouped)
         k0 = regroup_weights(K, 0, 0, on_vector)
+        turn_tokens(0, 1, x_grouped)
         v0 = regroup_weights(V, 0, 0, on_scalar)
-        k1 = regroup_weights(K, 1, 0, on_vector)
         quantise_weights(*k0)
+        k1 = regroup_weights(K, 1, 0, on_vector)
         quantise_window(0, x_grouped)
         quantise_weights(*k1)
         v1 = regroup_weights(V, 1, 0, on_vector)
@@ -201,7 +208,9 @@ def tile_localcontextprocessor_pa_kernel(tc, x, w_k, w_v, out):
         heads = project_keys(0, 0)
         quantise_weights(*v0)
         quantise_weights(*v1)
-        x_grouped = turn_window(1)
+        x_grouped = new_x_grouped()
+        for pair in range(2):
+            turn_tokens(1, pair, x_grouped)
         kf_grouped = finish_keys(heads)
         quantise_window(1, x_grouped)
         kf = quantise_tokens(kf_grouped, "kf")

@@ -34,9 +34,7 @@ def tile_localcontextprocessor_pa_kernel(tc, x, w_k, w_v, out):
 
     with tc.tile_pool(name="keep", bufs=1) as keep, tc.tile_pool(name="stage", bufs=2) as stage, tc.tile_pool(
         name="deep", bufs=4
-    ) as deep, tc.psum_pool(name="banks", bufs=7) as banks, tc.psum_pool(
-        name="context", bufs=1
-    ) as context, tc.manual_schedule():
+    ) as deep, tc.psum_pool(name="banks", bufs=8) as banks, tc.manual_schedule():
         x_tok = [
             [keep.tile([P, 2, FEATURES], BF16, name="x_tok%d_%d" % (w, pair)) for pair in range(2)] for w in range(WINDOWS)
         ]
@@ -152,20 +150,27 @@ def tile_localcontextprocessor_pa_kernel(tc, x, w_k, w_v, out):
                 nc.scalar.copy(out=v_grouped[:, i], in_=project(w, V, group, i))
             return v_grouped
 
-        def quantise_tokens(grouped, name):
+        def token_codes(name):
             codes = stage.tile([P, GROUP_COLS], U32, align_bytes=64, name=name + "_codes")
             scales = stage.tile([P, GROUP_COLS], U8, align_bytes=64, name=name + "_scales")
-            nc.vector.quantize_mx(
-                out=codes[:].bitcast(FP8X4), scales=scales[:], in_=grouped[:].rearrange("p i c j -> p (i c j)")
-            )
             return codes, scales
 
-        def contexts(w, group, kf, v):
-            ctx = context.tile([P, GROUP, HEAD], F32)
-            for i in range(GROUP):
+        def quantise_tokens(grouped, quantised, first=0, last=GROUP):
+            codes, scales = quantised
+            cols = slice(first * HEAD, last * HEAD)
+            nc.vector.quantize_mx(
+                out=codes[:, cols].bitcast(FP8X4),
+                scales=scales[:, cols],
+                in_=grouped[:, first:last].rearrange("p i c j -> p (i c j)"),
+            )
+            return quantised
+
+        def contexts(w, group, kf, v, first=0, last=GROUP):
+            ctx = banks.tile([P, last - first, HEAD], F32, tag="bank")
+            for i in range(first, last):
                 cols = slice(i * HEAD, (i + 1) * HEAD)
                 nc.tensor.matmul_mx(
-                    out=ctx[:, i, :],
+                    out=ctx[:, i - first, :],
                     lhsT=kf[0][:, cols].bitcast(FP8X4),
                     lhsT_scale=kf[1][:, cols],
                     rhs=v[0][:, cols].bitcast(FP8X4),
@@ -173,10 +178,10 @@ def tile_localcontextprocessor_pa_kernel(tc, x, w_k, w_v, out):
                     start=True,
                     stop=True,
                 )
-            ctx_sb = stage.tile([P, GROUP, HEAD], F32)
+            ctx_sb = deep.tile([P, last - first, HEAD], F32)
             nc.scalar.copy(out=ctx_sb[:], in_=ctx[:])
             nc.sync.dma_start(
-                out=out[w, group * GROUP : (group + 1) * GROUP].rearrange("h d e -> d h e"), in_=ctx_sb[:]
+                out=out[w, group * GROUP + first : group * GROUP + last].rearrange("h d e -> d h e"), in_=ctx_sb[:]
             )
 
         on_vector, on_scalar = nc.vector.tensor_copy, nc.scalar.copy
@@ -213,11 +218,11 @@ def tile_localcontextprocessor_pa_kernel(tc, x, w_k, w_v, out):
             turn_tokens(1, pair, x_grouped)
         kf_grouped = finish_keys(heads)
         quantise_window(1, x_grouped)
-        kf = quantise_tokens(kf_grouped, "kf")
+        kf = quantise_tokens(kf_grouped, token_codes("kf"))
         k0 = regroup_weights(K, 0, 1, on_vector)
         v_grouped = values(0, 0)
         k1 = regroup_weights(K, 1, 1, on_vector)
-        v = quantise_tokens(v_grouped, "v")
+        v = quantise_tokens(v_grouped, token_codes("v"))
         quantise_weights(*k0)
         done = (0, 0, kf, v)
 
@@ -226,18 +231,25 @@ def tile_localcontextprocessor_pa_kernel(tc, x, w_k, w_v, out):
         kf_grouped = finish_keys(heads)
         quantise_weights(*k1)
         v0 = regroup_weights(V, 0, 1, on_vector)
-        kf = quantise_tokens(kf_grouped, "kf")
+        kf = quantise_tokens(kf_grouped, token_codes("kf"))
         v_grouped = values(1, 0)
         v1 = regroup_weights(V, 1, 1, on_scalar)
         quantise_weights(*v0)
-        v = quantise_tokens(v_grouped, "v")
+        v = quantise_tokens(v_grouped, token_codes("v"))
         quantise_weights(*v1)
         done = (1, 0, kf, v)
 
-        for w in range(WINDOWS):
-            heads = project_keys(w, 1)
-            contexts(*done)
-            kf = quantise_tokens(finish_keys(heads), "kf")
-            v = quantise_tokens(values(w, 1), "v")
-            done = (w, 1, kf, v)
+        heads = project_keys(0, 1)
         contexts(*done)
+        kf = quantise_tokens(finish_keys(heads), token_codes("kf"))
+        v = quantise_tokens(values(0, 1), token_codes("v"))
+        done = (0, 1, kf, v)
+
+        heads = project_keys(1, 1)
+        contexts(*done)
+        kf = quantise_tokens(finish_keys(heads), token_codes("kf"))
+        v_grouped = values(1, 1)
+        v = token_codes("v")
+        for first, last in ((0, 2), (2, 3), (3, 4)):
+            quantise_tokens(v_grouped, v, first, last)
+            contexts(1, 1, kf, v, first, last)

@@ -45,8 +45,8 @@ def tile_localcontextprocessor_pa_kernel(tc, x, w_k, w_v, out):
             ]
             for m in (K, V)
         ]
-        x_codes = keep.tile([P, WINDOWS, PASSES, WINDOW], U32, align_bytes=64)
-        x_scales = keep.tile([P, WINDOWS, PASSES, WINDOW], U8, align_bytes=64)
+        x_codes = keep.tile([P, WINDOWS, 2, PASSES, WINDOW // 2], U32, align_bytes=64)
+        x_scales = keep.tile([P, WINDOWS, 2, PASSES, WINDOW // 2], U8, align_bytes=64)
         w_codes = [keep.tile([P, GROUPS, PASSES, GROUP_COLS], U32, align_bytes=64, name="w_codes%d" % m) for m in (K, V)]
         w_scales = [keep.tile([P, GROUPS, PASSES, GROUP_COLS], U8, align_bytes=64, name="w_scales%d" % m) for m in (K, V)]
 
@@ -63,7 +63,7 @@ def tile_localcontextprocessor_pa_kernel(tc, x, w_k, w_v, out):
                     in_=weights[m][first : first + 2 * P, cols].rearrange("(q e) c -> q e c", e=2),
                 )
 
-        def turn_tokens(w, pair, x_grouped):
+        def turn_tokens(w, pair, x_grouped, copies):
             x_words = x_tok[w][pair][:].rearrange("p a d -> p (a d)").bitcast(F32)
             for g in range(PASSES):
                 turned = banks.tile([P, 2, 2, P], F32, tag="bank")
@@ -71,29 +71,33 @@ def tile_localcontextprocessor_pa_kernel(tc, x, w_k, w_v, out):
                     for u in range(2):
                         first = ((a * PASSES + g) * 2 + u) * P
                         nc.tensor.transpose(turned[:, a, u, :], x_words[:, first : first + P], identity[:])
-                grouped_words = x_grouped[:, g, :].bitcast(F32)
-                nc.scalar.copy(
-                    out=grouped_words[:, pair * 4 * P : (pair + 1) * 4 * P].rearrange("q (a p u) -> q a p u", a=2, u=2),
+                grouped_words = x_grouped[:, pair, g, :].bitcast(F32)
+                copies[g](
+                    out=grouped_words.rearrange("q (a p u) -> q a p u", a=2, u=2),
                     in_=turned[:].rearrange("q a u p -> q a p u"),
                 )
 
         def new_x_grouped():
-            x_grouped = stage.tile([P, PASSES, PACK * WINDOW], BF16, align_bytes=64)
+            x_grouped = stage.tile([P, 2, PASSES, 2 * WINDOW], BF16, align_bytes=64)
             return x_grouped
 
-        def quantise_window(w, x_grouped):
+        def quantise_window(w, x_grouped, pairs=slice(0, 2)):
             nc.vector.quantize_mx(
-                out=x_codes[:, w].rearrange("q g n -> q (g n)").bitcast(FP8X4),
-                scales=x_scales[:, w].rearrange("q g n -> q (g n)"),
-                in_=x_grouped[:].rearrange("q g n -> q (g n)"),
+                out=x_codes[:, w, pairs].rearrange("q b g n -> q (b g n)").bitcast(FP8X4),
+                scales=x_scales[:, w, pairs].rearrange("q b g n -> q (b g n)"),
+                in_=x_grouped[:, pairs].rearrange("q b g n -> q (b g n)"),
             )
 
-        def regroup_weights(m, g, group, copy):
+        def regroup_weights(m, g, group, *shares):
             w_grouped = deep.tile([P, GROUP_COLS, PACK], BF16, align_bytes=64)
-            copy(
-                out=w_grouped[:].rearrange("q (c i) t -> q c t i", i=4),
-                in_=w_feat[m][g][group][:].rearrange("q t (c i) -> q c t i", i=4),
-            )
+            first = 0
+            for copy, width in shares:
+                cols = slice(first, first + width)
+                copy(
+                    out=w_grouped[:, cols, :].rearrange("q (c i) t -> q c t i", i=4),
+                    in_=w_feat[m][g][group][:, :, cols].rearrange("q t (c i) -> q c t i", i=4),
+                )
+                first += width
             return m, g, group, w_grouped
 
         def quantise_weights(m, g, group, w_grouped):
@@ -107,12 +111,13 @@ def tile_localcontextprocessor_pa_kernel(tc, x, w_k, w_v, out):
             bank = banks.tile([P, PACK, HEAD], F32, tag="bank")
             cols = slice(i * HEAD, (i + 1) * HEAD)
             for j in range(PACK):
-                toks = slice(j * P, (j + 1) * P)
+                pair, a = divmod(j, 2)
+                toks = slice(a * P, (a + 1) * P)
                 for g in range(PASSES):
                     nc.tensor.matmul_mx(
                         out=bank[:, j, :],
-                        lhsT=x_codes[:, w, g, toks].bitcast(FP8X4),
-                        lhsT_scale=x_scales[:, w, g, toks],
+                        lhsT=x_codes[:, w, pair, g, toks].bitcast(FP8X4),
+                        lhsT_scale=x_scales[:, w, pair, g, toks],
                         rhs=w_codes[m][:, group, g, cols].bitcast(FP8X4),
                         rhs_scale=w_scales[m][:, group, g, cols],
                         start=(g == 0),
@@ -185,10 +190,12 @@ def tile_localcontextprocessor_pa_kernel(tc, x, w_k, w_v, out):
             )
 
         on_vector, on_scalar = nc.vector.tensor_copy, nc.scalar.copy
+        all_vector, all_scalar = ((on_vector, GROUP_COLS),), ((on_scalar, GROUP_COLS),)
+        halves = ((on_scalar, GROUP_COLS // 2), (on_vector, GROUP_COLS // 2))
 
         for g in range(PASSES):
-            load_tokens(0, g)
             load_weights(K, g, 0)
+            load_tokens(0, g)
         for g in range(PASSES):
             load_weights(V, g, 0)
         for pair in range(2):
@@ -200,28 +207,29 @@ def tile_localcontextprocessor_pa_kernel(tc, x, w_k, w_v, out):
         make_identity(nc, identity[:])
 
         x_grouped = new_x_grouped()
-        turn_tokens(0, 0, x_grouped)
-        k0 = regroup_weights(K, 0, 0, on_vector)
-        turn_tokens(0, 1, x_grouped)
-        v0 = regroup_weights(V, 0, 0, on_scalar)
+        k0 = regroup_weights(K, 0, 0, *all_vector)
+        turn_tokens(0, 0, x_grouped, (on_vector, on_scalar))
         quantise_weights(*k0)
-        k1 = regroup_weights(K, 1, 0, on_vector)
-        quantise_window(0, x_grouped)
+        quantise_window(0, x_grouped, slice(0, 1))
+        k1 = regroup_weights(K, 1, 0, *halves)
+        turn_tokens(0, 1, x_grouped, (on_scalar, on_vector))
         quantise_weights(*k1)
-        v1 = regroup_weights(V, 1, 0, on_vector)
+        quantise_window(0, x_grouped, slice(1, 2))
+        v0 = regroup_weights(V, 0, 0, *halves)
+        v1 = regroup_weights(V, 1, 0, *all_vector)
 
         heads = project_keys(0, 0)
         quantise_weights(*v0)
         quantise_weights(*v1)
         x_grouped = new_x_grouped()
         for pair in range(2):
-            turn_tokens(1, pair, x_grouped)
+            turn_tokens(1, pair, x_grouped, (on_scalar, on_scalar))
         kf_grouped = finish_keys(heads)
         quantise_window(1, x_grouped)
         kf = quantise_tokens(kf_grouped, token_codes("kf"))
-        k0 = regroup_weights(K, 0, 1, on_vector)
+        k0 = regroup_weights(K, 0, 1, *halves)
         v_grouped = values(0, 0)
-        k1 = regroup_weights(K, 1, 1, on_vector)
+        k1 = regroup_weights(K, 1, 1, *all_vector)
         v = quantise_tokens(v_grouped, token_codes("v"))
         quantise_weights(*k0)
         done = (0, 0, kf, v)
@@ -230,10 +238,10 @@ def tile_localcontextprocessor_pa_kernel(tc, x, w_k, w_v, out):
         contexts(*done)
         kf_grouped = finish_keys(heads)
         quantise_weights(*k1)
-        v0 = regroup_weights(V, 0, 1, on_vector)
+        v0 = regroup_weights(V, 0, 1, *all_vector)
         kf = quantise_tokens(kf_grouped, token_codes("kf"))
         v_grouped = values(1, 0)
-        v1 = regroup_weights(V, 1, 1, on_scalar)
+        v1 = regroup_weights(V, 1, 1, *all_scalar)
         quantise_weights(*v0)
         v = quantise_tokens(v_grouped, token_codes("v"))
         quantise_weights(*v1)

@@ -22,6 +22,7 @@ PASSES = FEATURES // K_PASS
 GROUP = 4
 GROUPS = INNER // (GROUP * HEAD)
 GROUP_COLS = GROUP * HEAD
+GPSIMD_COLS = 320
 
 FLOPS = 2 * 2 * WINDOWS * WINDOW * FEATURES * INNER + 2 * WINDOWS * WINDOW * INNER * HEAD
 
@@ -88,9 +89,21 @@ def tile_localcontextprocessor_pa_kernel(tc, x, w_k, w_v, out):
                 in_=x_grouped[:, pairs].rearrange("q b g n -> q (b g n)"),
             )
 
-        def regroup_weights(m, g, group, *shares):
+        def on_gpsimd(out, in_):
+            nc.gpsimd.tensor_scalar(out=out, in0=in_, scalar1=one[:], scalar2=0.0, op0=ALU.mult, op1=ALU.add)
+
+        def beside_keys(m, g, group):
             w_grouped = deep.tile([P, GROUP_COLS, PACK], BF16, align_bytes=64)
-            first = 0
+
+            def start():
+                nc.vector.memset(one[:], 1.0)
+                regroup_weights(m, g, group, (on_gpsimd, GPSIMD_COLS), w_grouped=w_grouped)
+
+            return w_grouped, start
+
+        def regroup_weights(m, g, group, *shares, w_grouped=None, first=0):
+            if w_grouped is None:
+                w_grouped = deep.tile([P, GROUP_COLS, PACK], BF16, align_bytes=64)
             for copy, width in shares:
                 cols = slice(first, first + width)
                 copy(
@@ -127,25 +140,30 @@ def tile_localcontextprocessor_pa_kernel(tc, x, w_k, w_v, out):
 
         def project_keys(w, group):
             heads = []
+            exp_k = stage.tile([P, GROUP, HEAD, PACK], BF16)
             for i in range(GROUP):
                 k = project(w, K, group, i)
-                exp_k = deep.tile([P, HEAD, PACK], BF16)
-                nc.scalar.activation(out=exp_k[:], in_=k, func=ACT.Exp)
-                heads.append((k, exp_k))
-            return heads
+                nc.scalar.activation(out=exp_k[:, i], in_=k, func=ACT.Exp)
+                heads.append(k)
+            return heads, exp_k
 
-        def finish_keys(heads):
+        def finish_keys(keys, together=1, beside=None):
             kf_grouped = stage.tile([P, GROUP, HEAD, PACK], BF16, align_bytes=64)
 
-            def clamp(i):
-                nc.vector.tensor_scalar_min(out=heads[i][1][:], in0=heads[i][1][:], scalar1=1.0)
+            heads, exp_k = keys
+
+            def clamp(first):
+                some = exp_k[:, first : first + together]
+                nc.vector.tensor_scalar_min(out=some, in0=some, scalar1=1.0)
 
             clamp(0)
+            if beside:
+                beside()
             for i in range(GROUP):
-                if i + 1 < GROUP:
-                    clamp(i + 1)
+                if i % together == 0 and i + together < GROUP:
+                    clamp(i + together)
                 nc.vector.scalar_tensor_tensor(
-                    out=kf_grouped[:, i], in0=heads[i][0], scalar=1.0, in1=heads[i][1][:], op0=ALU.add, op1=ALU.max
+                    out=kf_grouped[:, i], in0=heads[i], scalar=1.0, in1=exp_k[:, i], op0=ALU.add, op1=ALU.max
                 )
             return kf_grouped
 
@@ -203,6 +221,7 @@ def tile_localcontextprocessor_pa_kernel(tc, x, w_k, w_v, out):
         for m in (K, V):
             for g in range(PASSES):
                 load_weights(m, g, 1)
+        one = keep.tile([P, 1], F32)
         identity = keep.tile([P, P], F32)
         make_identity(nc, identity[:])
 
@@ -212,7 +231,7 @@ def tile_localcontextprocessor_pa_kernel(tc, x, w_k, w_v, out):
         quantise_weights(*k0)
         quantise_window(0, x_grouped, slice(0, 1))
         k1 = regroup_weights(K, 1, 0, *halves)
-        turn_tokens(0, 1, x_grouped, (on_scalar, on_vector))
+        turn_tokens(0, 1, x_grouped, (on_scalar, on_scalar))
         quantise_weights(*k1)
         quantise_window(0, x_grouped, slice(1, 2))
         v0 = regroup_weights(V, 0, 0, *halves)
@@ -224,10 +243,11 @@ def tile_localcontextprocessor_pa_kernel(tc, x, w_k, w_v, out):
         x_grouped = new_x_grouped()
         for pair in range(2):
             turn_tokens(1, pair, x_grouped, (on_scalar, on_scalar))
-        kf_grouped = finish_keys(heads)
+        w_grouped, start = beside_keys(K, 0, 1)
+        kf_grouped = finish_keys(heads, GROUP, start)
         quantise_window(1, x_grouped)
         kf = quantise_tokens(kf_grouped, token_codes("kf"))
-        k0 = regroup_weights(K, 0, 1, *halves)
+        k0 = regroup_weights(K, 0, 1, (on_scalar, GROUP_COLS - GPSIMD_COLS), w_grouped=w_grouped, first=GPSIMD_COLS)
         v_grouped = values(0, 0)
         k1 = regroup_weights(K, 1, 1, *all_vector)
         v = quantise_tokens(v_grouped, token_codes("v"))
@@ -236,12 +256,13 @@ def tile_localcontextprocessor_pa_kernel(tc, x, w_k, w_v, out):
 
         heads = project_keys(1, 0)
         contexts(*done)
-        kf_grouped = finish_keys(heads)
+        w_grouped, start = beside_keys(V, 1, 1)
+        kf_grouped = finish_keys(heads, GROUP, start)
         quantise_weights(*k1)
-        v0 = regroup_weights(V, 0, 1, *all_vector)
+        v0 = regroup_weights(V, 0, 1, *halves)
         kf = quantise_tokens(kf_grouped, token_codes("kf"))
         v_grouped = values(1, 0)
-        v1 = regroup_weights(V, 1, 1, *all_scalar)
+        v1 = regroup_weights(V, 1, 1, (on_scalar, GROUP_COLS - GPSIMD_COLS), w_grouped=w_grouped, first=GPSIMD_COLS)
         quantise_weights(*v0)
         v = quantise_tokens(v_grouped, token_codes("v"))
         quantise_weights(*v1)

@@ -89,15 +89,19 @@ def tile_localcontextprocessor_pa_kernel(tc, x, w_k, w_v, out):
                 in_=x_grouped[:, pairs].rearrange("q b g n -> q (b g n)"),
             )
 
-        def on_gpsimd(out, in_):
-            nc.gpsimd.tensor_scalar(out=out, in0=in_, scalar1=one[:], scalar2=0.0, op0=ALU.mult, op1=ALU.add)
-
         def beside_keys(m, g, group):
             w_grouped = deep.tile([P, GROUP_COLS, PACK], BF16, align_bytes=64)
 
             def start():
                 nc.vector.memset(one[:], 1.0)
-                regroup_weights(m, g, group, (on_gpsimd, GPSIMD_COLS), w_grouped=w_grouped)
+                nc.gpsimd.tensor_scalar(
+                    out=w_grouped[:, :GPSIMD_COLS, :],
+                    in0=w_feat[m][g][group][:, :, :GPSIMD_COLS].rearrange("q t c -> q c t"),
+                    scalar1=one[:],
+                    scalar2=0.0,
+                    op0=ALU.mult,
+                    op1=ALU.add,
+                )
 
             return w_grouped, start
 

@@ -144,30 +144,29 @@ def tile_localcontextprocessor_pa_kernel(tc, x, w_k, w_v, out):
 
         def project_keys(w, group):
             heads = []
-            exp_k = stage.tile([P, GROUP, HEAD, PACK], BF16)
             for i in range(GROUP):
                 k = project(w, K, group, i)
-                nc.scalar.activation(out=exp_k[:, i], in_=k, func=ACT.Exp)
-                heads.append(k)
-            return heads, exp_k
+                exp_k = deep.tile([P, HEAD, PACK], BF16)
+                nc.scalar.activation(out=exp_k[:], in_=k, func=ACT.Exp)
+                heads.append((k, exp_k))
+            return heads
 
-        def finish_keys(keys, together=1, beside=None):
+        def finish_keys(heads, beside=None):
             kf_grouped = stage.tile([P, GROUP, HEAD, PACK], BF16, align_bytes=64)
 
-            heads, exp_k = keys
+            def clamp(i):
+                nc.vector.tensor_scalar_min(out=heads[i][1][:], in0=heads[i][1][:], scalar1=1.0)
 
-            def clamp(first):
-                some = exp_k[:, first : first + together]
-                nc.vector.tensor_scalar_min(out=some, in0=some, scalar1=1.0)
-
-            clamp(0)
+            ahead = GROUP if beside else 1
+            for i in range(ahead):
+                clamp(i)
             if beside:
                 beside()
             for i in range(GROUP):
-                if i % together == 0 and i + together < GROUP:
-                    clamp(i + together)
+                if i + ahead < GROUP:
+                    clamp(i + ahead)
                 nc.vector.scalar_tensor_tensor(
-                    out=kf_grouped[:, i], in0=heads[i], scalar=1.0, in1=exp_k[:, i], op0=ALU.add, op1=ALU.max
+                    out=kf_grouped[:, i], in0=heads[i][0], scalar=1.0, in1=heads[i][1][:], op0=ALU.add, op1=ALU.max
                 )
             return kf_grouped
 
@@ -248,7 +247,7 @@ def tile_localcontextprocessor_pa_kernel(tc, x, w_k, w_v, out):
         for pair in range(2):
             turn_tokens(1, pair, x_grouped, (on_scalar, on_scalar))
         w_grouped, start = beside_keys(K, 0, 1)
-        kf_grouped = finish_keys(heads, GROUP, start)
+        kf_grouped = finish_keys(heads, start)
         quantise_window(1, x_grouped)
         kf = quantise_tokens(kf_grouped, token_codes("kf"))
         k0 = regroup_weights(K, 0, 1, (on_scalar, GROUP_COLS - GPSIMD_COLS), w_grouped=w_grouped, first=GPSIMD_COLS)
@@ -261,7 +260,7 @@ def tile_localcontextprocessor_pa_kernel(tc, x, w_k, w_v, out):
         heads = project_keys(1, 0)
         contexts(*done)
         w_grouped, start = beside_keys(V, 1, 1)
-        kf_grouped = finish_keys(heads, GROUP, start)
+        kf_grouped = finish_keys(heads, start)
         quantise_weights(*k1)
         v0 = regroup_weights(V, 0, 1, *halves)
         kf = quantise_tokens(kf_grouped, token_codes("kf"))

@@ -22,7 +22,7 @@ PASSES = FEATURES // K_PASS
 GROUP = 4
 GROUPS = INNER // (GROUP * HEAD)
 GROUP_COLS = GROUP * HEAD
-GPSIMD_COLS = 320
+GPSIMD_COLS = 384
 
 FLOPS = 2 * 2 * WINDOWS * WINDOW * FEATURES * INNER + 2 * WINDOWS * WINDOW * INNER * HEAD
 
@@ -232,8 +232,8 @@ def tile_localcontextprocessor_pa_kernel(tc, x, w_k, w_v, out):
         k0 = regroup_weights(K, 0, 0, *all_vector)
         turn_tokens(0, 0, x_grouped, (on_vector, on_scalar))
         quantise_weights(*k0)
-        quantise_window(0, x_grouped, slice(0, 1))
         k1 = regroup_weights(K, 1, 0, *halves)
+        quantise_window(0, x_grouped, slice(0, 1))
         turn_tokens(0, 1, x_grouped, (on_scalar, on_scalar))
         quantise_weights(*k1)
         quantise_window(0, x_grouped, slice(1, 2))
@@ -273,13 +273,22 @@ def tile_localcontextprocessor_pa_kernel(tc, x, w_k, w_v, out):
 
         heads = project_keys(0, 1)
         contexts(*done)
-        kf = quantise_tokens(finish_keys(heads), token_codes("kf"))
-        v = quantise_tokens(values(0, 1), token_codes("v"))
+        kf = token_codes("kf")
+        kf_grouped = finish_keys(heads)
+        for first in (0, 2):
+            quantise_tokens(kf_grouped, kf, first, first + 2)
+        v_grouped = values(0, 1)
+        v = token_codes("v")
+        for first in (0, 2):
+            quantise_tokens(v_grouped, v, first, first + 2)
         done = (0, 1, kf, v)
 
         heads = project_keys(1, 1)
         contexts(*done)
-        kf = quantise_tokens(finish_keys(heads), token_codes("kf"))
+        kf = token_codes("kf")
+        kf_grouped = finish_keys(heads)
+        for first in (0, 2):
+            quantise_tokens(kf_grouped, kf, first, first + 2)
         v_grouped = values(1, 1)
         v = token_codes("v")
         for first, last in ((0, 2), (2, 3), (3, 4)):

@@ -22,7 +22,7 @@ PASSES = FEATURES // K_PASS
 GROUP = 4
 GROUPS = INNER // (GROUP * HEAD)
 GROUP_COLS = GROUP * HEAD
-GPSIMD_COLS = 384
+GPSIMD_COLS = 256
 
 FLOPS = 2 * 2 * WINDOWS * WINDOW * FEATURES * INNER + 2 * WINDOWS * WINDOW * INNER * HEAD
 
@@ -181,6 +181,12 @@ def tile_localcontextprocessor_pa_kernel(tc, x, w_k, w_v, out):
             scales = stage.tile([P, GROUP_COLS], U8, align_bytes=64, name=name + "_scales")
             return codes, scales
 
+        def warm_up(products):
+            bank = banks.tile([P, GROUP_COLS], F32, tag="bank")
+            some_x = x_tok[0][0][:, 0, :]
+            for product in range(products):
+                nc.tensor.matmul(out=bank[:], lhsT=some_x[:, :P], rhs=some_x[:, :GROUP_COLS], start=True, stop=True)
+
         def quantise_tokens(grouped, quantised, first=0, last=GROUP):
             codes, scales = quantised
             cols = slice(first * HEAD, last * HEAD)
@@ -231,10 +237,12 @@ def tile_localcontextprocessor_pa_kernel(tc, x, w_k, w_v, out):
         x_grouped = new_x_grouped()
         k0 = regroup_weights(K, 0, 0, *all_vector)
         turn_tokens(0, 0, x_grouped, (on_vector, on_scalar))
+        warm_up(3)
         quantise_weights(*k0)
         k1 = regroup_weights(K, 1, 0, *halves)
         quantise_window(0, x_grouped, slice(0, 1))
         turn_tokens(0, 1, x_grouped, (on_scalar, on_scalar))
+        warm_up(3)
         quantise_weights(*k1)
         quantise_window(0, x_grouped, slice(1, 2))
         v0 = regroup_weights(V, 0, 0, *halves)
@@ -250,7 +258,7 @@ def tile_localcontextprocessor_pa_kernel(tc, x, w_k, w_v, out):
         kf_grouped = finish_keys(heads, start)
         quantise_window(1, x_grouped)
         kf = quantise_tokens(kf_grouped, token_codes("kf"))
-        k0 = regroup_weights(K, 0, 1, (on_scalar, GROUP_COLS - GPSIMD_COLS), w_grouped=w_grouped, first=GPSIMD_COLS)
+        k0 = regroup_weights(K, 0, 1, (on_scalar, 128), (on_vector, 128), w_grouped=w_grouped, first=GPSIMD_COLS)
         v_grouped = values(0, 0)
         k1 = regroup_weights(K, 1, 1, *all_vector)
         v = quantise_tokens(v_grouped, token_codes("v"))

@@ -51,9 +51,13 @@ def tile_localcontextprocessor_pa_kernel(tc, x, w_k, w_v, out):
         w_codes = [keep.tile([P, GROUPS, PASSES, GROUP_COLS], U32, align_bytes=64, name="w_codes%d" % m) for m in (K, V)]
         w_scales = [keep.tile([P, GROUPS, PASSES, GROUP_COLS], U8, align_bytes=64, name="w_scales%d" % m) for m in (K, V)]
 
-        def load_tokens(w, pair):
+        def load_tokens(w, pair, together=2):
             window = x_rows[w * WINDOW : (w + 1) * WINDOW, :].rearrange("(p j) d -> p j d", j=PACK)
-            nc.sync.dma_start(out=x_tok[w][pair][:], in_=window[:, 2 * pair : 2 * pair + 2, :])
+            for a in range(0, 2, together):
+                nc.sync.dma_start(
+                    out=x_tok[w][pair][:, a : a + together, :],
+                    in_=window[:, 2 * pair + a : 2 * pair + a + together, :],
+                )
 
         def load_weights(m, g, group):
             cols = slice(group * GROUP_COLS, (group + 1) * GROUP_COLS)
@@ -66,16 +70,16 @@ def tile_localcontextprocessor_pa_kernel(tc, x, w_k, w_v, out):
 
         def turn_tokens(w, pair, x_grouped, copies):
             x_words = x_tok[w][pair][:].rearrange("p a d -> p (a d)").bitcast(F32)
-            for g in range(PASSES):
-                turned = banks.tile([P, 2, 2, P], F32, tag="bank")
-                for a in range(2):
+            grouped_words = x_grouped[:, pair].bitcast(F32)
+            for a in range(2):
+                turned = banks.tile([P, PASSES, 2, P], F32, tag="bank")
+                for g in range(PASSES):
                     for u in range(2):
                         first = ((a * PASSES + g) * 2 + u) * P
-                        nc.tensor.transpose(turned[:, a, u, :], x_words[:, first : first + P], identity[:])
-                grouped_words = x_grouped[:, pair, g, :].bitcast(F32)
-                copies[g](
-                    out=grouped_words.rearrange("q (a p u) -> q a p u", a=2, u=2),
-                    in_=turned[:].rearrange("q a u p -> q a p u"),
+                        nc.tensor.transpose(turned[:, g, u, :], x_words[:, first : first + P], identity[:])
+                copies[a](
+                    out=grouped_words[:, :, a * 2 * P : (a + 1) * 2 * P].rearrange("q g (p u) -> q g p u", u=2),
+                    in_=turned[:].rearrange("q g u p -> q g p u"),
                 )
 
         def new_x_grouped():
@@ -115,6 +119,21 @@ def tile_localcontextprocessor_pa_kernel(tc, x, w_k, w_v, out):
                     in_=w_feat[m][g][group][:, :, cols].rearrange("q t (c i) -> q c t i", i=4),
                 )
                 first += width
+            return m, g, group, w_grouped
+
+        def regroup_half_on_tensor(m, g, group, w_grouped, first):
+            bank = banks.tile([P, GROUP_COLS // 2, PACK], BF16, tag="bank")
+            cols = slice(first, first + GROUP_COLS // 2)
+            for u in range(2):
+                rows = slice(2 * u, 2 * u + 2)
+                nc.tensor.matmul(
+                    out=bank[:, :, rows],
+                    lhsT=identity_bf[:],
+                    rhs=w_feat[m][g][group][:, rows, cols].rearrange("q t c -> q c t"),
+                    start=True,
+                    stop=True,
+                )
+            nc.scalar.copy(out=w_grouped[:, cols, :], in_=bank[:])
             return m, g, group, w_grouped
 
         def quantise_weights(m, g, group, w_grouped):
@@ -222,7 +241,7 @@ def tile_localcontextprocessor_pa_kernel(tc, x, w_k, w_v, out):
 
         for g in range(PASSES):
             load_weights(K, g, 0)
-            load_tokens(0, g)
+            load_tokens(0, g, 1)
         for g in range(PASSES):
             load_weights(V, g, 0)
         for pair in range(2):
@@ -233,6 +252,8 @@ def tile_localcontextprocessor_pa_kernel(tc, x, w_k, w_v, out):
         one = keep.tile([P, 1], F32)
         identity = keep.tile([P, P], F32)
         make_identity(nc, identity[:])
+        identity_bf = keep.tile([P, P], BF16)
+        make_identity(nc, identity_bf[:])
 
         x_grouped = new_x_grouped()
         k0 = regroup_weights(K, 0, 0, *all_vector)
@@ -273,7 +294,7 @@ def tile_localcontextprocessor_pa_kernel(tc, x, w_k, w_v, out):
         v0 = regroup_weights(V, 0, 1, *halves)
         kf = quantise_tokens(kf_grouped, token_codes("kf"))
         v_grouped = values(1, 0)
-        v1 = regroup_weights(V, 1, 1, (on_scalar, GROUP_COLS - GPSIMD_COLS), w_grouped=w_grouped, first=GPSIMD_COLS)
+        v1 = regroup_half_on_tensor(V, 1, 1, w_grouped, GROUP_COLS // 2)
         quantise_weights(*v0)
         v = quantise_tokens(v_grouped, token_codes("v"))
         quantise_weights(*v1)

import concourse.mybir as mybir
from concourse.masks import make_identity

F32 = mybir.dt.float32
BF16 = mybir.dt.bfloat16
U32 = mybir.dt.uint32
U8 = mybir.dt.uint8
FP8X4 = mybir.dt.float8_e4m3fn_x4
ALU = mybir.AluOpType
ACT = mybir.ActivationFunctionType

P = 128
PACK = 4
K_PASS = P * PACK

FEATURES = 1024
INNER = 1024
HEAD = 128
WINDOW = 512
WINDOWS = 2
PASSES = FEATURES // K_PASS
GROUP = 4
GROUPS = INNER // (GROUP * HEAD)
GROUP_COLS = GROUP * HEAD
GPSIMD_COLS = 256

FLOPS = 2 * 2 * WINDOWS * WINDOW * FEATURES * INNER + 2 * WINDOWS * WINDOW * INNER * HEAD


def tile_localcontextprocessor_pa_kernel(tc, x, w_k, w_v, out):
    nc = tc.nc
    x_rows = x.flatten_outer_dims()
    weights = (w_k, w_v)
    K, V = 0, 1

    with tc.tile_pool(name="keep", bufs=1) as keep, tc.tile_pool(name="stage", bufs=2) as stage, tc.tile_pool(
        name="deep", bufs=4
    ) as deep, tc.psum_pool(name="banks", bufs=8) as banks, tc.manual_schedule():
        x_tok = [
            [keep.tile([P, 2, FEATURES], BF16, name="x_tok%d_%d" % (w, pair)) for pair in range(2)] for w in range(WINDOWS)
        ]
        w_feat = [
            [
                [keep.tile([P, PACK, GROUP_COLS], BF16, name="w_feat%d_%d_%d" % (m, g, group)) for group in range(GROUPS)]
                for g in range(PASSES)
            ]
            for m in (K, V)
        ]
        x_codes = keep.tile([P, WINDOWS, 2, PASSES, WINDOW // 2], U32, align_bytes=64)
        x_scales = keep.tile([P, WINDOWS, 2, PASSES, WINDOW // 2], U8, align_bytes=64)
        w_codes = [keep.tile([P, GROUPS, PASSES, GROUP_COLS], U32, align_bytes=64, name="w_codes%d" % m) for m in (K, V)]
        w_scales = [keep.tile([P, GROUPS, PASSES, GROUP_COLS], U8, align_bytes=64, name="w_scales%d" % m) for m in (K, V)]

        def load_tokens(w, pair, together=2):
            window = x_rows[w * WINDOW : (w + 1) * WINDOW, :].rearrange("(p j) d -> p j d", j=PACK)
            for a in range(0, 2, together):
                nc.sync.dma_start(
                    out=x_tok[w][pair][:, a : a + together, :],
                    in_=window[:, 2 * pair + a : 2 * pair + a + together, :],
                )

        def load_weights(m, g, group):
            cols = slice(group * GROUP_COLS, (group + 1) * GROUP_COLS)
            for u in range(2):
                first = g * K_PASS + u * 2 * P
                nc.sync.dma_start(
                    out=w_feat[m][g][group][:, 2 * u : 2 * u + 2, :],
                    in_=weights[m][first : first + 2 * P, cols].rearrange("(q e) c -> q e c", e=2),
                )

        def turn_tokens(w, pair, x_grouped, copies):
            x_words = x_tok[w][pair][:].rearrange("p a d -> p (a d)").bitcast(F32)
            grouped_words = x_grouped[:, pair].bitcast(F32)
            for a in range(2):
                turned = banks.tile([P, PASSES, 2, P], F32, tag="bank")
                for g in range(PASSES):
                    for u in range(2):
                        first = ((a * PASSES + g) * 2 + u) * P
                        nc.tensor.transpose(turned[:, g, u, :], x_words[:, first : first + P], identity[:])
                copies[a](
                    out=grouped_words[:, :, a * 2 * P : (a + 1) * 2 * P].rearrange("q g (p u) -> q g p u", u=2),
                    in_=turned[:].rearrange("q g u p -> q g p u"),
                )

        def new_x_grouped():
            x_grouped = stage.tile([P, 2, PASSES, 2 * WINDOW], BF16, align_bytes=64)
            return x_grouped

        def quantise_window(w, x_grouped, pairs=slice(0, 2)):
            nc.vector.quantize_mx(
                out=x_codes[:, w, pairs].rearrange("q b g n -> q (b g n)").bitcast(FP8X4),
                scales=x_scales[:, w, pairs].rearrange("q b g n -> q (b g n)"),
                in_=x_grouped[:, pairs].rearrange("q b g n -> q (b g n)"),
            )

        def beside_keys(m, g, group):
            w_grouped = deep.tile([P, GROUP_COLS, PACK], BF16, align_bytes=64)

            def start():
                nc.vector.memset(one[:], 1.0)
                nc.gpsimd.tensor_scalar(
                    out=w_grouped[:, :GPSIMD_COLS, :],
                    in0=w_feat[m][g][group][:, :, :GPSIMD_COLS].rearrange("q t c -> q c t"),
                    scalar1=one[:],
                    scalar2=0.0,
                    op0=ALU.mult,
                    op1=ALU.add,
                )

            return w_grouped, start

        def regroup_weights(m, g, group, *shares, w_grouped=None, first=0):
            if w_grouped is None:
                w_grouped = deep.tile([P, GROUP_COLS, PACK], BF16, align_bytes=64)
            for copy, width in shares:
                cols = slice(first, first + width)
                copy(
                    out=w_grouped[:, cols, :].rearrange("q (c i) t -> q c t i", i=4),
                    in_=w_feat[m][g][group][:, :, cols].rearrange("q t (c i) -> q c t i", i=4),
                )
                first += width
            return m, g, group, w_grouped

        def regroup_half_on_tensor(m, g, group, w_grouped, first):
            bank = banks.tile([P, GROUP_COLS // 2, PACK], BF16, tag="bank")
            cols = slice(first, first + GROUP_COLS // 2)
            for u in range(2):
                rows = slice(2 * u, 2 * u + 2)
                nc.tensor.matmul(
                    out=bank[:, :, rows],
                    lhsT=identity_bf[:],
                    rhs=w_feat[m][g][group][:, rows, cols].rearrange("q t c -> q c t"),
                    start=True,
                    stop=True,
                )
            nc.scalar.copy(out=w_grouped[:, cols, :], in_=bank[:])
            return m, g, group, w_grouped

        def quantise_weights(m, g, group, w_grouped):
            nc.vector.quantize_mx(
                out=w_codes[m][:, group, g, :].bitcast(FP8X4),
                scales=w_scales[m][:, group, g, :],
                in_=w_grouped[:].rearrange("q c t -> q (c t)"),
            )

        def project(w, m, group, i):
            bank = banks.tile([P, PACK, HEAD], F32, tag="bank")
            cols = slice(i * HEAD, (i + 1) * HEAD)
            for j in range(PACK):
                pair, a = divmod(j, 2)
                toks = slice(a * P, (a + 1) * P)
                for g in range(PASSES):
                    nc.tensor.matmul_mx(
                        out=bank[:, j, :],
                        lhsT=x_codes[:, w, pair, g, toks].bitcast(FP8X4),
                        lhsT_scale=x_scales[:, w, pair, g, toks],
                        rhs=w_codes[m][:, group, g, cols].bitcast(FP8X4),
                        rhs_scale=w_scales[m][:, group, g, cols],
                        start=(g == 0),
                        stop=(g == PASSES - 1),
                    )
            return bank[:].rearrange("p j c -> p c j")

        def project_keys(w, group):
            heads = []
            for i in range(GROUP):
                k = project(w, K, group, i)
                exp_k = deep.tile([P, HEAD, PACK], BF16)
                nc.scalar.activation(out=exp_k[:], in_=k, func=ACT.Exp)
                heads.append((k, exp_k))
            return heads

        def finish_keys(heads, beside=None):
            kf_grouped = stage.tile([P, GROUP, HEAD, PACK], BF16, align_bytes=64)

            def clamp(i):
                nc.vector.tensor_scalar_min(out=heads[i][1][:], in0=heads[i][1][:], scalar1=1.0)

            ahead = GROUP if beside else 1
            for i in range(ahead):
                clamp(i)
            if beside:
                beside()
            for i in range(GROUP):
                if i + ahead < GROUP:
                    clamp(i + ahead)
                nc.vector.scalar_tensor_tensor(
                    out=kf_grouped[:, i], in0=heads[i][0], scalar=1.0, in1=heads[i][1][:], op0=ALU.add, op1=ALU.max
                )
            return kf_grouped

        def values(w, group):
            v_grouped = stage.tile([P, GROUP, HEAD, PACK], BF16, align_bytes=64)
            for i in range(GROUP):
                nc.scalar.copy(out=v_grouped[:, i], in_=project(w, V, group, i))
            return v_grouped

        def token_codes(name):
            codes = stage.tile([P, GROUP_COLS], U32, align_bytes=64, name=name + "_codes")
            scales = stage.tile([P, GROUP_COLS], U8, align_bytes=64, name=name + "_scales")
            return codes, scales

        def warm_up(products):
            bank = banks.tile([P, GROUP_COLS], F32, tag="bank")
            some_x = x_tok[0][0][:, 0, :]
            for product in range(products):
                nc.tensor.matmul(out=bank[:], lhsT=some_x[:, :P], rhs=some_x[:, :GROUP_COLS], start=True, stop=True)

        def quantise_tokens(grouped, quantised, first=0, last=GROUP):
            codes, scales = quantised
            cols = slice(first * HEAD, last * HEAD)
            nc.vector.quantize_mx(
                out=codes[:, cols].bitcast(FP8X4),
                scales=scales[:, cols],
                in_=grouped[:, first:last].rearrange("p i c j -> p (i c j)"),
            )
            return quantised

        def contexts(w, group, kf, v, first=0, last=GROUP):
            ctx = banks.tile([P, last - first, HEAD], F32, tag="bank")
            for i in range(first, last):
                cols = slice(i * HEAD, (i + 1) * HEAD)
                nc.tensor.matmul_mx(
                    out=ctx[:, i - first, :],
                    lhsT=kf[0][:, cols].bitcast(FP8X4),
                    lhsT_scale=kf[1][:, cols],
                    rhs=v[0][:, cols].bitcast(FP8X4),
                    rhs_scale=v[1][:, cols],
                    start=True,
                    stop=True,
                )
            ctx_sb = deep.tile([P, last - first, HEAD], F32)
            nc.scalar.copy(out=ctx_sb[:], in_=ctx[:])
            nc.sync.dma_start(
                out=out[w, group * GROUP + first : group * GROUP + last].rearrange("h d e -> d h e"), in_=ctx_sb[:]
            )

        on_vector, on_scalar = nc.vector.tensor_copy, nc.scalar.copy
        all_vector, all_scalar = ((on_vector, GROUP_COLS),), ((on_scalar, GROUP_COLS),)
        halves = ((on_scalar, GROUP_COLS // 2), (on_vector, GROUP_COLS // 2))

        for g in range(PASSES):
            load_weights(K, g, 0)
            load_tokens(0, g, 1)
        for g in range(PASSES):
            load_weights(V, g, 0)
        for pair in range(2):
            load_tokens(1, pair)
        for m in (K, V):
            for g in range(PASSES):
                load_weights(m, g, 1)
        one = keep.tile([P, 1], F32)
        identity = keep.tile([P, P], F32)
        make_identity(nc, identity[:])
        identity_bf = keep.tile([P, P], BF16)
        make_identity(nc, identity_bf[:])

        x_grouped = new_x_grouped()
        k0 = regroup_weights(K, 0, 0, *all_vector)
        turn_tokens(0, 0, x_grouped, (on_vector, on_scalar))
        warm_up(3)
        quantise_weights(*k0)
        k1 = regroup_weights(K, 1, 0, *halves)
        quantise_window(0, x_grouped, slice(0, 1))
        turn_tokens(0, 1, x_grouped, (on_scalar, on_scalar))
        warm_up(3)
        quantise_weights(*k1)
        quantise_window(0, x_grouped, slice(1, 2))
        v0 = regroup_weights(V, 0, 0, *halves)
        v1 = regroup_weights(V, 1, 0, *all_vector)

        heads = project_keys(0, 0)
        quantise_weights(*v0)
        quantise_weights(*v1)
        x_grouped = new_x_grouped()
        for pair in range(2):
            turn_tokens(1, pair, x_grouped, (on_scalar, on_scalar))
        w_grouped, start = beside_keys(K, 0, 1)
        kf_grouped = finish_keys(heads, start)
        quantise_window(1, x_grouped)
        kf = quantise_tokens(kf_grouped, token_codes("kf"))
        k0 = regroup_weights(K, 0, 1, (on_scalar, 128), (on_vector, 128), w_grouped=w_grouped, first=GPSIMD_COLS)
        v_grouped = values(0, 0)
        k1 = regroup_weights(K, 1, 1, *all_vector)
        v = quantise_tokens(v_grouped, token_codes("v"))
        quantise_weights(*k0)
        done = (0, 0, kf, v)

        heads = project_keys(1, 0)
        contexts(*done)
        w_grouped, start = beside_keys(V, 1, 1)
        kf_grouped = finish_keys(heads, start)
        quantise_weights(*k1)
        v0 = regroup_weights(V, 0, 1, *halves)
        kf = quantise_tokens(kf_grouped, token_codes("kf"))
        v_grouped = values(1, 0)
        v1 = regroup_half_on_tensor(V, 1, 1, w_grouped, GROUP_COLS // 2)
        quantise_weights(*v0)
        v = quantise_tokens(v_grouped, token_codes("v"))
        quantise_weights(*v1)
        done = (1, 0, kf, v)

        heads = project_keys(0, 1)
        contexts(*done)
        kf = token_codes("kf")
        kf_grouped = finish_keys(heads)
        for first in (0, 2):
            quantise_tokens(kf_grouped, kf, first, first + 2)
        v_grouped = values(0, 1)
        v = token_codes("v")
        for first in (0, 2):
            quantise_tokens(v_grouped, v, first, first + 2)
        done = (0, 1, kf, v)

        heads = project_keys(1, 1)
        contexts(*done)
        kf = token_codes("kf")
        kf_grouped = finish_keys(heads)
        for first in (0, 2):
            quantise_tokens(kf_grouped, kf, first, first + 2)
        v_grouped = values(1, 1)
        v = token_codes("v")
        for first, last in ((0, 2), (2, 3), (3, 4)):
            quantise_tokens(v_grouped, v, first, last)
            contexts(1, 1, kf, v, first, last)
